import numpy as np
import ml_dtypes


def mxq(x, axis, fmt="e4m3"):
    dtype, down = {"e4m3": (ml_dtypes.float8_e4m3fn, 7), "e5m2": (ml_dtypes.float8_e5m2, 14)}[fmt]
    v = np.moveaxis(np.asarray(x, np.float32).astype(ml_dtypes.bfloat16).astype(np.float64), axis, -1)
    blocks = v.reshape(v.shape[:-1] + (-1, 32))
    amax = np.abs(blocks).max(-1, keepdims=True)
    byte = np.maximum(np.where(amax > 0, np.frexp(amax)[1] - 1 + 127, 0) - down, 1)
    scale = np.exp2(byte - 127.0)
    codes = (blocks / scale).astype(np.float32).astype(dtype).astype(np.float64)
    return np.moveaxis((codes * scale).reshape(v.shape), -1, axis)


WIDE = False


def mx_kscale(k):
    if not WIDE:
        return np.ones(k)
    levels = np.array([10, -10, 5, -5, 0])
    if k % 512:
        return np.exp2(np.random.permutation(np.resize(levels, k // 32))).repeat(32)
    a = np.empty((k // 512, 16))
    for p in range(k // 512):
        a[p, :8] = np.random.permutation(np.resize(levels, 8))
        for g in range(8):
            far = levels[np.abs(levels - a[p, g]) >= 10]
            a[p, g + 8] = far[np.random.randint(len(far))]
    return np.exp2(a.ravel()).repeat(32)


BF16 = ml_dtypes.bfloat16


def bf(x):
    return np.asarray(x, np.float32).astype(BF16)


def f64(x):
    return np.asarray(x).astype(np.float64)


B, IN_F, OUT_F = 1024, 1024, 4096
IN_Q = IN_F // 4
OUT_Q = OUT_F // 4


def setup_inputs():
    s = mx_kscale(B)[:, None]
    u = mx_kscale(OUT_Q)
    scale = 1.0 / np.sqrt(IN_Q)
    inp = {"x": bf(f64(bf(np.random.standard_normal((B, IN_F)))) * s)}
    for name in ["rr", "ri", "rj", "rk"]:
        w0 = bf(np.random.uniform(-scale, scale, (OUT_Q, IN_Q)))
        inp["W_" + name] = bf(f64(w0) / u[:, None])
    for name in ["rr", "ri", "rj", "rk"]:
        inp["b_" + name] = bf(np.random.standard_normal(OUT_Q) * 0.5)
    g = np.random.standard_normal((B, OUT_F)) * np.exp2(np.random.randint(-6, 1, (B, 1))) * 2.0
    inp["grad_out"] = bf(g / s * np.tile(u, 4))
    return inp


def chunks(a, n):
    return a[:, :n], a[:, n:2 * n], a[:, 2 * n:3 * n], a[:, 3 * n:]


def reference(x, W_rr, W_ri, W_rj, W_rk, b_rr, b_ri, b_rj, b_rk, grad_out):
    g = f64(grad_out)
    gr, gi, gj, gk = chunks(mxq(g, 1, "e5m2"), OUT_Q)
    wr = mxq(f64(W_rr), 0, "e4m3")
    wi = mxq(f64(W_ri), 0, "e4m3")
    wj = mxq(f64(W_rj), 0, "e4m3")
    wk = mxq(f64(W_rk), 0, "e4m3")
    dx_r = gr @ wr + gi @ wi + gj @ wj + gk @ wk
    dx_i = gi @ wr - gr @ wi + gk @ wj - gj @ wk
    dx_j = gj @ wr - gk @ wi - gr @ wj + gi @ wk
    dx_k = gk @ wr + gj @ wi - gi @ wj - gr @ wk
    dx = np.concatenate([dx_r, dx_i, dx_j, dx_k], axis=1)
    tr, ti, tj, tk = chunks(mxq(g, 0, "e5m2"), OUT_Q)
    xr, xi, xj, xk = chunks(mxq(f64(x), 0, "e4m3"), IN_Q)
    dw = ti.T @ xr - tr.T @ xi - tk.T @ xj + tj.T @ xk
    return dx, dw

@@ -1,0 +1,422 @@
+from contextlib import ExitStack
+
+import concourse.mybir as mybir
+from concourse.masks import make_identity
+
+FLOPS = 2 * 20 * 1024 * 1024 * 256
+BYTES = 2 * (1024 * 1024 + 4 * 1024 * 256 + 1024 * 4096) + 4 * (1024 * 1024 + 1024 * 256)
+
+F32 = mybir.dt.float32
+BF16 = mybir.dt.bfloat16
+U32 = mybir.dt.uint32
+U8 = mybir.dt.uint8
+E4 = mybir.dt.float8_e4m3fn_x4
+E5 = mybir.dt.float8_e5m2_x4
+COPY = mybir.ActivationFunctionType.Copy
+MULT = mybir.AluOpType.mult
+
+P = 128
+PACK = 4
+KP = P * PACK
+CH = 1024
+IQ = 256
+
+POS_BLOCK = {"ri": 0, "rr": 1, "rk": 3, "rj": 4}
+NEG_BLOCK = {"ri": 2, "rk": 5, "rj": 6}
+W_ORDER = ("ri", "rr", "rk", "rj")
+WIN_RI = (1, 0, 4, 3)
+WIN_KJ = (5, 6, 0, 1)
+X_FOR_G = (1, 0, 3, 2)
+X_SIGN = (1, -1, -1, 1)
+
+SORTED_FROM = 4
+FAST = True
+FILL = ((2, 1, 3), (2, 1, 3), (2, 1, 3), (2, 1, 3), (2, 2, 3))
+TAIL = (2, 1)
+RJ = "VS"
+
+
+def tile_qdense_v_kernel(tc, x, W_rr, W_ri, W_rj, W_rk, b_rr, b_ri, b_rj, b_rk, grad_out, out_0, out_1):
+    nc = tc.nc
+    weights = {"rr": W_rr, "ri": W_ri, "rj": W_rj, "rk": W_rk}
+
+    with ExitStack() as ctx:
+        keep = ctx.enter_context(tc.tile_pool(name="keep", bufs=1))
+        work = ctx.enter_context(tc.tile_pool(name="work", bufs=1))
+        psum = ctx.enter_context(tc.psum_pool(name="psum", bufs=1))
+        ctx.enter_context(tc.manual_schedule())
+
+        def sb(pool, shape, dtype, tag, bufs=1):
+            return pool.tile(shape, dtype, name=tag, tag=tag, bufs=bufs, align_bytes=64)
+
+        warm = sb(keep, [P, 2], F32, "warm")
+        nc.gpsimd.memset(warm[:], 0.0)
+        nc.scalar.activation(out=warm[:, 1:2], in_=warm[:, 0:1], func=COPY, scale=-1.0)
+        ident = sb(keep, [P, P], F32, "ident")
+        make_identity(nc, ident[:])
+
+        g_raw = [sb(keep, [P, PACK, 4 * CH], BF16, "g_raw%d" % g) for g in range(2)]
+        w_raw = [sb(work, [P, 4, PACK, IQ], BF16, "raw8", bufs=2) for q in range(2)]
+        x_raw = []
+
+        def load_w(q):
+            for m, name in enumerate(W_ORDER):
+                rows = weights[name][q * KP : (q + 1) * KP, :]
+                nc.sync.dma_start(out=w_raw[q][:, m, :, :], in_=rows.rearrange("(p j) w -> p j w", j=PACK))
+
+        def load_g(t, pieces):
+            g, j = divmod(t, PACK)
+            rows = grad_out[g * KP : (g + 1) * KP, :].rearrange("(p j) w -> p j w", j=PACK)
+            n = 4 * CH // pieces
+            for c in range(pieces):
+                cols = slice(c * n, (c + 1) * n)
+                nc.sync.dma_start(out=g_raw[g][:, j, cols], in_=rows[:, j, cols])
+
+        load_w(0)
+        load_g(0, 4)
+        load_g(1, 4)
+        load_w(1)
+        for t in range(2, 8):
+            load_g(t, 2)
+
+        def load_x(g):
+            tile = sb(work, [P, PACK, 4 * IQ], BF16, "raw8", bufs=2)
+            rows = x[g * KP : (g + 1) * KP, :].rearrange("(p j) w -> p j w", j=PACK)
+            nc.sync.dma_start(out=tile[:], in_=rows)
+            x_raw.append(tile)
+
+        def interleave(engine, dst, src, sign=1):
+            if FAST:
+                o = dst.rearrange("p (c i) t -> p c t i", i=4)
+                i = src.rearrange("p t (c i) -> p c t i", i=4)
+            else:
+                o = dst
+                i = src.rearrange("p t c -> p c t")
+            if engine == "V":
+                if sign > 0:
+                    nc.vector.tensor_copy(out=o, in_=i)
+                else:
+                    nc.vector.tensor_scalar(out=o, in0=i, scalar1=-1.0, scalar2=None, op0=MULT)
+            elif sign > 0:
+                nc.scalar.copy(out=o, in_=i)
+            else:
+                nc.scalar.activation(out=o, in_=i, func=COPY, scale=-1.0)
+
+        def quantize(codes, scales, src, fmt):
+            nc.vector.quantize_mx(out=codes.bitcast(fmt), scales=scales, in_=src)
+
+        w_il = [sb(work, [P, 7, IQ, PACK], BF16, "big16", bufs=2) for q in range(2)]
+        w_codes = [sb(keep, [P, 8 * IQ], U32, "w_codes%d" % q) for q in range(2)]
+        w_scales = [sb(keep, [P, 8 * IQ], U8, "w_scales%d" % q) for q in range(2)]
+
+        def w_interleave(q, name, sign, engine):
+            block = (POS_BLOCK if sign > 0 else NEG_BLOCK)[name]
+            interleave(engine, w_il[q][:, block, :, :], w_raw[q][:, W_ORDER.index(name), :, :], sign)
+
+        def w_quantize(q, first, count, src):
+            cols = slice(first * IQ, (first + count) * IQ)
+            quantize(
+                w_codes[q][:, cols],
+                w_scales[q][:, cols],
+                w_il[q][:, src : src + count, :, :].rearrange("p b w j -> p (b w j)"),
+                E4,
+            )
+
+        def w_negate(q, name):
+            nc.vector.tensor_scalar(
+                out=w_il[q][:, NEG_BLOCK[name], :, :],
+                in0=w_il[q][:, POS_BLOCK[name], :, :],
+                scalar1=-1.0,
+                scalar2=None,
+                op0=MULT,
+            )
+
+        gt = {}
+        gt_codes = {}
+        gt_scales = {}
+        xbanks = {}
+        sorted_words = {}
+
+        def sort_words(t):
+            g, j = divmod(t, PACK)
+            sorted_words[t] = sb(work, [P, 4 * CH // 2], F32, "sorted", bufs=1)
+            nc.vector.tensor_copy(
+                out=sorted_words[t][:].rearrange("p (s u n) -> p s u n", u=2, n=P),
+                in_=g_raw[g][:, j, :].bitcast(F32).rearrange("p (s n u) -> p s u n", u=2, n=P),
+            )
+
+        def transposes(t, chunks=range(4)):
+            g, j = divmod(t, PACK)
+            words = sorted_words[t][:] if t in sorted_words else g_raw[g][:, j, :].bitcast(F32)
+            for c in chunks:
+                bank = psum.tile([P, 2, 2, P], F32, name="xb%d" % c, tag="xb%d" % c, bufs=1)
+                xbanks[t, c] = bank
+                for q in range(2):
+                    for u in range(2):
+                        base = 2 * P * (2 * c + q)
+                        if t in sorted_words:
+                            src = words[:, base + u * P : base + (u + 1) * P]
+                        else:
+                            src = words[:, base + u : base + 2 * P : 2]
+                        nc.tensor.transpose(bank[:, q, u, :], src, ident[:])
+
+        def bank_out(t, c, engine):
+            if t not in gt:
+                gt[t] = sb(work, [P, 8, P, PACK], BF16, "gt", bufs=2)
+            dst = gt[t][:, 2 * c : 2 * c + 2, :, :].rearrange("p s n i -> p s (n i)").bitcast(F32)
+            dst = dst.rearrange("p s (n u) -> p s n u", u=2)
+            src = xbanks[t, c][:].rearrange("p s u n -> p s n u")
+            if engine == "V":
+                nc.vector.tensor_copy(out=dst, in_=src)
+            else:
+                nc.scalar.copy(out=dst, in_=src)
+
+        def gt_quantize(t, first, count):
+            if t not in gt_codes:
+                gt_codes[t] = sb(work, [P, 8 * P], U32, "gt_codes", bufs=3)
+                gt_scales[t] = sb(work, [P, 8 * P], U8, "gt_scales", bufs=3)
+            cols = slice(first * P, (first + count) * P)
+            quantize(
+                gt_codes[t][:, cols],
+                gt_scales[t][:, cols],
+                gt[t][:, first : first + count, :, :].rearrange("p s n i -> p (s n i)"),
+                E5,
+            )
+
+        obanks = {}
+
+        def multiply(t, halves, windows=(0, 1)):
+            for b in windows:
+                if (t, b) not in obanks:
+                    tag = "ob%d%d" % (t % 2, b)
+                    obanks[t, b] = psum.tile([P, 512], F32, name=tag, tag=tag, bufs=1)
+                for c in range(4):
+                    for q in halves:
+                        s = slice((2 * c + q) * P, (2 * c + q + 1) * P)
+                        first = (WIN_RI, WIN_KJ)[b][c] * IQ
+                        w = slice(first, first + 512)
+                        nc.tensor.matmul_mx(
+                            out=obanks[t, b][:],
+                            lhsT=gt_codes[t][:, s].bitcast(E5),
+                            lhsT_scale=gt_scales[t][:, s],
+                            rhs=w_codes[q][:, w].bitcast(E4),
+                            rhs_scale=w_scales[q][:, w],
+                            start=(c == 0 and q == 0),
+                            stop=(c == 3 and q == 1),
+                        )
+
+        o_sb = {}
+
+        def copy(engine, out, in_):
+            if engine == "V":
+                nc.vector.tensor_copy(out=out, in_=in_)
+            else:
+                nc.scalar.copy(out=out, in_=in_)
+
+        def out0(t, b, engine):
+            g, j = divmod(t, PACK)
+            if t not in o_sb:
+                o_sb[t] = sb(work, [P, 4 * IQ], F32, "o_sb", bufs=3)
+            if b == 0:
+                copy(engine, o_sb[t][:, 0:512], obanks[t, 0][:])
+            else:
+                copy(engine, o_sb[t][:, 768:1024], obanks[t, 1][:, 0:256])
+                copy(engine, o_sb[t][:, 512:768], obanks[t, 1][:, 256:512])
+            rows = out_0[g * KP : (g + 1) * KP, :].rearrange("(p j) w -> p j w", j=PACK)
+            cols = slice(b * 512, (b + 1) * 512)
+            nc.sync.dma_start(out=rows[:, j, cols], in_=o_sb[t][:, cols])
+
+        tok_codes = []
+        tok_scales = []
+        x_codes = []
+        x_scales = []
+        il = {}
+
+        def tok_interleave(u, engine):
+            g, part = divmod(u, 8)
+            il[u] = sb(work, [P, 512, PACK], BF16, "il", bufs=4)
+            interleave(engine, il[u][:], g_raw[g][:, :, part * 512 : (part + 1) * 512])
+
+        def tok_quantize(u):
+            g, part = divmod(u, 8)
+            if part == 0:
+                if g == 0:
+                    tok_codes.append(sb(keep, [P, 4 * CH], U32, "tok_codes0"))
+                else:
+                    tok_codes.append(sb(work, [P, 4 * CH], U32, "big16", bufs=2))
+                tok_scales.append(sb(keep, [P, 4 * CH], U8, "tok_scales%d" % g))
+            cols = slice(part * 512, (part + 1) * 512)
+            quantize(tok_codes[g][:, cols], tok_scales[g][:, cols], il[u][:].rearrange("p n i -> p (n i)"), E5)
+
+        x_il = {}
+
+        def x_interleave(g, c, engine):
+            pair = c // 2
+            if c % 2 == 0:
+                x_il[g, pair] = sb(work, [P, 512, PACK], BF16, "il", bufs=4)
+            half = slice((c % 2) * IQ, (c % 2 + 1) * IQ)
+            interleave(engine, x_il[g, pair][:, half, :], x_raw[g][:, :, c * IQ : (c + 1) * IQ], X_SIGN[c])
+
+        def x_quantize(g, pair):
+            if g == 0 and pair == 0:
+                x_codes.append(sb(work, [P, 2, 4 * IQ], U32, "big16", bufs=2))
+                x_scales.append(sb(keep, [P, 2, 4 * IQ], U8, "x_scales"))
+            cols = slice(pair * 512, (pair + 1) * 512)
+            quantize(
+                x_codes[0][:, g, cols], x_scales[0][:, g, cols], x_il[g, pair][:].rearrange("p n i -> p (n i)"), E4
+            )
+
+        nbanks = {}
+
+        def grad_w(g, chunks):
+            for c in chunks:
+                for i in range(2):
+                    for h in range(2):
+                        k = 2 * i + h
+                        if k not in nbanks:
+                            nbanks[k] = psum.tile([P, 512], F32, name="xb%d" % k, tag="xb%d" % k, bufs=1)
+                        xs = slice(X_FOR_G[c] * IQ + i * P, X_FOR_G[c] * IQ + (i + 1) * P)
+                        gs = slice(c * CH + h * 512, c * CH + (h + 1) * 512)
+                        nc.tensor.matmul_mx(
+                            out=nbanks[k][:],
+                            lhsT=x_codes[0][:, g, xs].bitcast(E4),
+                            lhsT_scale=x_scales[0][:, g, xs],
+                            rhs=tok_codes[g][:, gs].bitcast(E5),
+                            rhs_scale=tok_scales[g][:, gs],
+                            start=(g == 0 and c == 0),
+                            stop=(g == 1 and c == 3),
+                        )
+
+        o1t = {}
+        o1 = []
+
+        def grad_w_out(k, engine):
+            o1t[k] = sb(work, [P, 512], F32, "il", bufs=4)
+            copy(engine, o1t[k][:], nbanks[k][:])
+
+        def grad_w_store(n, bank_tag, engine):
+            bank = psum.tile([P, 2, 2, P], F32, name=bank_tag, tag=bank_tag, bufs=1)
+            h = n // 2
+            for b in range(2):
+                for i in range(2):
+                    f = ((n % 2) * 2 + b) * P
+                    nc.tensor.transpose(bank[:, b, i, :], o1t[2 * i + h][:, f : f + P], ident[:])
+            if n == 0:
+                o1.append(sb(work, [P, 4, 2, 2, P], F32, "gt", bufs=2))
+            res = o1[0][:, n, :, :, :]
+            copy(engine, res, bank[:])
+            rows = out_1[n * 2 * P : (n + 1) * 2 * P, :].rearrange("(b p) i -> p b i", p=P)
+            nc.sync.dma_start(out=rows, in_=res.rearrange("p b i n -> p b (i n)"))
+
+        items = [("t", u) for u in range(8)] + [("x", c) for c in range(4)]
+        items += [("t", u) for u in range(8, 16)] + [("x", c) for c in range(4, 8)]
+        pending = []
+
+        def fill(engine, count=1):
+            share = 2 * count
+            while items and share > 0:
+                kind, n = items.pop(0)
+                share -= 2 if kind == "t" else 1
+                if kind == "t":
+                    tok_interleave(n, engine)
+                    pending.append((kind, n))
+                else:
+                    x_interleave(n // 4, n % 4, engine)
+                    if n % 2 == 1:
+                        pending.append((kind, n // 2))
+
+        def drain(count=1):
+            for k in range(count):
+                if not pending:
+                    return
+                kind, n = pending.pop(0)
+                if kind == "t":
+                    tok_quantize(n)
+                else:
+                    x_quantize(n // 2, n % 2)
+
+        def w_half(q):
+            w_interleave(q, "ri", 1, "V")
+            w_interleave(q, "ri", -1, "S")
+            w_interleave(q, "rr", 1, "V")
+            w_interleave(q, "rk", 1, "V")
+            w_quantize(q, 0, 2, 0)
+            w_interleave(q, "rk", -1, "S")
+            w_interleave(q, "rj", 1, RJ[q])
+            w_quantize(q, 2, 1, 2)
+            w_negate(q, "rj")
+            w_quantize(q, 3, 2, 3)
+            w_quantize(q, 7, 1, 3)
+            w_quantize(q, 5, 2, 5)
+
+        def banks_out(t, engine="S"):
+            for c in range(4):
+                bank_out(t, c, engine)
+
+        w_half(0)
+        transposes(0)
+        banks_out(0)
+        transposes(1)
+        gt_quantize(0, 0, 4)
+        gt_quantize(0, 4, 4)
+        banks_out(1)
+        multiply(0, (0,))
+        gt_quantize(1, 0, 4)
+        gt_quantize(1, 4, 4)
+        w_half(1)
+        load_x(0)
+        load_x(1)
+        multiply(1, (0,))
+        transposes(2)
+        fill("V", 1)
+        banks_out(2)
+        multiply(0, (1,))
+        fill("V", 1)
+        gt_quantize(2, 0, 4)
+        drain(1)
+        gt_quantize(2, 4, 4)
+        if 3 >= SORTED_FROM:
+            sort_words(3)
+        fill("S", 1)
+        multiply(1, (1,))
+        out0(0, 0, "S")
+        out0(0, 1, "S")
+
+        for t in range(2, 7):
+            nv, ns, nd = FILL[t - 2]
+            transposes(t + 1)
+            fill("V")
+            drain()
+            banks_out(t + 1)
+            if t == 2:
+                out0(1, 0, "S")
+            out0(t - 1, 1, "S")
+            if t + 2 >= SORTED_FROM and t + 2 < 8:
+                sort_words(t + 2)
+            gt_quantize(t + 1, 0, 4)
+            drain()
+            fill("V", nv - 1)
+            gt_quantize(t + 1, 4, 4)
+            drain(nd - 2)
+            if t == 6:
+                grad_w(0, range(4))
+            multiply(t, (0, 1), (0,))
+            fill("S", ns)
+            out0(t, 0, "S")
+            multiply(t, (0, 1), (1,))
+        fill("V", TAIL[0])
+        drain(1)
+        fill("S", TAIL[1])
+        out0(6, 1, "S")
+        drain(8)
+        fill("V", 4)
+        drain(8)
+        grad_w(1, range(4))
+        for k in range(4):
+            grad_w_out(k, "SV"[k % 2])
+        multiply(7, (0, 1), (0,))
+        for n in range(4):
+            grad_w_store(n, ("ob00", "ob01", "xb0", "xb1")[n], "VS"[n % 2])
+        out0(7, 0, "S")
+        multiply(7, (0, 1), (1,))
+        out0(7, 1, "V")

@@ -29,10 +29,10 @@ WIN_KJ = (5, 6, 0, 1)
 X_FOR_G = (1, 0, 3, 2)
 X_SIGN = (1, -1, -1, 1)
 
-SORTED_FROM = 4
+SORTED_FROM = 3
 FAST = True
-FILL = ((2, 1, 3), (2, 1, 3), (2, 1, 3), (2, 1, 3), (2, 2, 3))
-TAIL = (2, 1)
+FILL = ((2, 1, 3), (1, 1, 3), (2, 1, 3), (1, 1, 3), (2, 1, 3))
+TAIL = (1, 1, 1, 1)
 RJ = "VS"
 
 
@@ -268,13 +268,12 @@ def tile_qdense_v_kernel(tc, x, W_rr, W_ri, W_rj, W_rk, b_rr, b_ri, b_rj, b_rk, 
 
         nbanks = {}
 
-        def grad_w(g, chunks):
-            for c in chunks:
-                for i in range(2):
-                    for h in range(2):
-                        k = 2 * i + h
-                        if k not in nbanks:
-                            nbanks[k] = psum.tile([P, 512], F32, name="xb%d" % k, tag="xb%d" % k, bufs=1)
+        def grad_w(h):
+            for i in range(2):
+                k = 2 * i + h
+                nbanks[k] = psum.tile([P, 512], F32, name="xb%d" % k, tag="xb%d" % k, bufs=1)
+                for g in range(2):
+                    for c in range(4):
                         xs = slice(X_FOR_G[c] * IQ + i * P, X_FOR_G[c] * IQ + (i + 1) * P)
                         gs = slice(c * CH + h * 512, c * CH + (h + 1) * 512)
                         nc.tensor.matmul_mx(
@@ -308,8 +307,9 @@ def tile_qdense_v_kernel(tc, x, W_rr, W_ri, W_rj, W_rk, b_rr, b_ri, b_rj, b_rk, 
             rows = out_1[n * 2 * P : (n + 1) * 2 * P, :].rearrange("(b p) i -> p b i", p=P)
             nc.sync.dma_start(out=rows, in_=res.rearrange("p b i n -> p b (i n)"))
 
-        items = [("t", u) for u in range(8)] + [("x", c) for c in range(4)]
-        items += [("t", u) for u in range(8, 16)] + [("x", c) for c in range(4, 8)]
+        items = [("t", u) for u in (0, 2, 4, 6, 1, 3, 5, 7)] + [("x", c) for c in range(4)]
+        items += [("t", u) for u in (8, 10, 12, 14)] + [("x", c) for c in range(4, 8)]
+        items += [("t", u) for u in (9, 11, 13, 15)]
         pending = []
 
         def fill(engine, count=1):
@@ -368,15 +368,12 @@ def tile_qdense_v_kernel(tc, x, W_rr, W_ri, W_rj, W_rk, b_rr, b_ri, b_rj, b_rk, 
         load_x(1)
         multiply(1, (0,))
         transposes(2)
-        fill("V", 1)
+        sort_words(3)
         banks_out(2)
         multiply(0, (1,))
         fill("V", 1)
         gt_quantize(2, 0, 4)
-        drain(1)
         gt_quantize(2, 4, 4)
-        if 3 >= SORTED_FROM:
-            sort_words(3)
         fill("S", 1)
         multiply(1, (1,))
         out0(0, 0, "S")
@@ -391,32 +388,36 @@ def tile_qdense_v_kernel(tc, x, W_rr, W_ri, W_rj, W_rk, b_rr, b_ri, b_rj, b_rk, 
             if t == 2:
                 out0(1, 0, "S")
             out0(t - 1, 1, "S")
-            if t + 2 >= SORTED_FROM and t + 2 < 8:
+            if t + 2 < 8:
                 sort_words(t + 2)
             gt_quantize(t + 1, 0, 4)
             drain()
             fill("V", nv - 1)
             gt_quantize(t + 1, 4, 4)
             drain(nd - 2)
-            if t == 6:
-                grad_w(0, range(4))
             multiply(t, (0, 1), (0,))
             fill("S", ns)
             out0(t, 0, "S")
             multiply(t, (0, 1), (1,))
+        multiply(7, (0, 1), (0,))
         fill("V", TAIL[0])
         drain(1)
         fill("S", TAIL[1])
         out0(6, 1, "S")
-        drain(8)
-        fill("V", 4)
-        drain(8)
-        grad_w(1, range(4))
-        for k in range(4):
-            grad_w_out(k, "SV"[k % 2])
-        multiply(7, (0, 1), (0,))
-        for n in range(4):
-            grad_w_store(n, ("ob00", "ob01", "xb0", "xb1")[n], "VS"[n % 2])
+        drain(2)
+        fill("V", TAIL[2])
+        drain(2)
         out0(7, 0, "S")
         multiply(7, (0, 1), (1,))
-        out0(7, 1, "V")
+        fill("S", TAIL[3])
+        fill("V", 9)
+        drain(9)
+        out0(7, 1, "S")
+        grad_w(0)
+        grad_w(1)
+        grad_w_out(0, "V")
+        grad_w_out(2, "S")
+        grad_w_out(1, "V")
+        grad_w_out(3, "S")
+        for n in range(4):
+            grad_w_store(n, ("ob00", "ob01", "ob10", "ob11")[n], "VS"[n % 2])

@@ -33,7 +33,8 @@ SORTED_FROM = 3
 FAST = True
 FILL = ((2, 1, 3), (1, 1, 3), (2, 1, 3), (1, 1, 3), (2, 1, 3))
 TAIL = (1, 1, 1, 1)
-RJ = "VS"
+CHUNKS = ((0, 1, 2, 3), (2, 3, 0, 1))
+O1_BANKS = ("ob00", "ob01", "ob10", "ob11", "xb0", "xb2", "ob00", "ob01")
 
 
 def tile_qdense_v_kernel(tc, x, W_rr, W_ri, W_rj, W_rk, b_rr, b_ri, b_rj, b_rk, grad_out, out_0, out_1):
@@ -47,7 +48,7 @@ def tile_qdense_v_kernel(tc, x, W_rr, W_ri, W_rj, W_rk, b_rr, b_ri, b_rj, b_rk, 
         ctx.enter_context(tc.manual_schedule())
 
         def sb(pool, shape, dtype, tag, bufs=1):
-            return pool.tile(shape, dtype, name=tag, tag=tag, bufs=bufs, align_bytes=64)
+            return pool.tile(shape, dtype, name=tag, tag=tag, bufs=bufs, align_bytes=256)
 
         warm = sb(keep, [P, 2], F32, "warm")
         nc.gpsimd.memset(warm[:], 0.0)
@@ -59,25 +60,28 @@ def tile_qdense_v_kernel(tc, x, W_rr, W_ri, W_rj, W_rk, b_rr, b_ri, b_rj, b_rk, 
         w_raw = [sb(work, [P, 4, PACK, IQ], BF16, "raw8", bufs=2) for q in range(2)]
         x_raw = []
 
-        def load_w(q):
-            for m, name in enumerate(W_ORDER):
+        def load_w(q, first, last):
+            for m in range(first, last):
+                name = W_ORDER[m]
                 rows = weights[name][q * KP : (q + 1) * KP, :]
                 nc.sync.dma_start(out=w_raw[q][:, m, :, :], in_=rows.rearrange("(p j) w -> p j w", j=PACK))
 
-        def load_g(t, pieces):
+        def load_g(t, pieces, first, last):
             g, j = divmod(t, PACK)
             rows = grad_out[g * KP : (g + 1) * KP, :].rearrange("(p j) w -> p j w", j=PACK)
             n = 4 * CH // pieces
-            for c in range(pieces):
+            for c in range(first, last):
                 cols = slice(c * n, (c + 1) * n)
                 nc.sync.dma_start(out=g_raw[g][:, j, cols], in_=rows[:, j, cols])
 
-        load_w(0)
-        load_g(0, 4)
-        load_g(1, 4)
-        load_w(1)
+        load_w(0, 0, 3)
+        load_g(0, 4, 0, 1)
+        load_w(0, 3, 4)
+        load_g(0, 4, 1, 4)
+        load_g(1, 4, 0, 4)
+        load_w(1, 0, 4)
         for t in range(2, 8):
-            load_g(t, 2)
+            load_g(t, 1, 0, 1)
 
         def load_x(g):
             tile = sb(work, [P, PACK, 4 * IQ], BF16, "raw8", bufs=2)
@@ -139,7 +143,7 @@ def tile_qdense_v_kernel(tc, x, W_rr, W_ri, W_rj, W_rk, b_rr, b_ri, b_rj, b_rk, 
 
         def sort_words(t):
             g, j = divmod(t, PACK)
-            sorted_words[t] = sb(work, [P, 4 * CH // 2], F32, "sorted", bufs=1)
+            sorted_words[t] = sb(work, [P, 4 * CH // 2], F32, "sorted", bufs=2)
             nc.vector.tensor_copy(
                 out=sorted_words[t][:].rearrange("p (s u n) -> p s u n", u=2, n=P),
                 in_=g_raw[g][:, j, :].bitcast(F32).rearrange("p (s n u) -> p s u n", u=2, n=P),
@@ -190,7 +194,7 @@ def tile_qdense_v_kernel(tc, x, W_rr, W_ri, W_rj, W_rk, b_rr, b_ri, b_rj, b_rk, 
                 if (t, b) not in obanks:
                     tag = "ob%d%d" % (t % 2, b)
                     obanks[t, b] = psum.tile([P, 512], F32, name=tag, tag=tag, bufs=1)
-                for c in range(4):
+                for n, c in enumerate(CHUNKS[b]):
                     for q in halves:
                         s = slice((2 * c + q) * P, (2 * c + q + 1) * P)
                         first = (WIN_RI, WIN_KJ)[b][c] * IQ
@@ -201,8 +205,8 @@ def tile_qdense_v_kernel(tc, x, W_rr, W_ri, W_rj, W_rk, b_rr, b_ri, b_rj, b_rk, 
                             lhsT_scale=gt_scales[t][:, s],
                             rhs=w_codes[q][:, w].bitcast(E4),
                             rhs_scale=w_scales[q][:, w],
-                            start=(c == 0 and q == 0),
-                            stop=(c == 3 and q == 1),
+                            start=(n == 0 and q == 0),
+                            stop=(n == 3 and q == 1),
                         )
 
         o_sb = {}
@@ -293,19 +297,17 @@ def tile_qdense_v_kernel(tc, x, W_rr, W_ri, W_rj, W_rk, b_rr, b_ri, b_rj, b_rk, 
             o1t[k] = sb(work, [P, 512], F32, "il", bufs=4)
             copy(engine, o1t[k][:], nbanks[k][:])
 
-        def grad_w_store(n, bank_tag, engine):
-            bank = psum.tile([P, 2, 2, P], F32, name=bank_tag, tag=bank_tag, bufs=1)
-            h = n // 2
-            for b in range(2):
-                for i in range(2):
-                    f = ((n % 2) * 2 + b) * P
-                    nc.tensor.transpose(bank[:, b, i, :], o1t[2 * i + h][:, f : f + P], ident[:])
-            if n == 0:
-                o1.append(sb(work, [P, 4, 2, 2, P], F32, "gt", bufs=2))
-            res = o1[0][:, n, :, :, :]
-            copy(engine, res, bank[:])
-            rows = out_1[n * 2 * P : (n + 1) * 2 * P, :].rearrange("(b p) i -> p b i", p=P)
-            nc.sync.dma_start(out=rows, in_=res.rearrange("p b i n -> p b (i n)"))
+        def grad_w_store(f, engine):
+            tag = O1_BANKS[f]
+            bank = psum.tile([P, 2, P], F32, name=tag, tag=tag, bufs=1)
+            h, part = divmod(f, 4)
+            for i in range(2):
+                nc.tensor.transpose(bank[:, i, :], o1t[2 * i + h][:, part * P : (part + 1) * P], ident[:])
+            if f == 0:
+                o1.append(sb(work, [P, 8, 2 * P], F32, "gt", bufs=2))
+            res = o1[0][:, f, :]
+            copy(engine, res, bank[:].rearrange("p i n -> p (i n)"))
+            nc.sync.dma_start(out=out_1[f * P : (f + 1) * P, :], in_=res)
 
         items = [("t", u) for u in (0, 2, 4, 6, 1, 3, 5, 7)] + [("x", c) for c in range(4)]
         items += [("t", u) for u in (8, 10, 12, 14)] + [("x", c) for c in range(4, 8)]
@@ -335,40 +337,49 @@ def tile_qdense_v_kernel(tc, x, W_rr, W_ri, W_rj, W_rk, b_rr, b_ri, b_rj, b_rk, 
                 else:
                     x_quantize(n // 2, n % 2)
 
-        def w_half(q):
-            w_interleave(q, "ri", 1, "V")
-            w_interleave(q, "ri", -1, "S")
-            w_interleave(q, "rr", 1, "V")
-            w_interleave(q, "rk", 1, "V")
-            w_quantize(q, 0, 2, 0)
-            w_interleave(q, "rk", -1, "S")
-            w_interleave(q, "rj", 1, RJ[q])
-            w_quantize(q, 2, 1, 2)
-            w_negate(q, "rj")
-            w_quantize(q, 3, 2, 3)
-            w_quantize(q, 7, 1, 3)
-            w_quantize(q, 5, 2, 5)
-
         def banks_out(t, engine="S"):
             for c in range(4):
                 bank_out(t, c, engine)
 
-        w_half(0)
+        w_interleave(0, "ri", 1, "V")
+        w_interleave(0, "ri", -1, "S")
+        w_interleave(0, "rr", 1, "V")
+        w_interleave(0, "rk", 1, "V")
+        w_quantize(0, 0, 2, 0)
+        w_interleave(0, "rk", -1, "S")
+        w_interleave(0, "rj", 1, "V")
+        w_quantize(0, 2, 1, 2)
+        w_negate(0, "rj")
         transposes(0)
         banks_out(0)
-        transposes(1)
         gt_quantize(0, 0, 4)
+        w_quantize(0, 3, 2, 3)
         gt_quantize(0, 4, 4)
+        w_quantize(0, 7, 1, 3)
+        w_quantize(0, 5, 2, 5)
+        transposes(1)
         banks_out(1)
         multiply(0, (0,))
         gt_quantize(1, 0, 4)
+        w_interleave(1, "ri", 1, "V")
         gt_quantize(1, 4, 4)
-        w_half(1)
+        w_interleave(1, "rj", 1, "S")
+        w_interleave(1, "rr", 1, "V")
+        w_interleave(1, "ri", -1, "S")
+        w_interleave(1, "rk", 1, "V")
+        w_interleave(1, "rk", -1, "S")
+        w_quantize(1, 0, 2, 0)
+        w_quantize(1, 3, 2, 3)
+        w_negate(1, "rj")
+        w_quantize(1, 7, 1, 3)
+        w_quantize(1, 2, 1, 2)
+        w_quantize(1, 5, 2, 5)
         load_x(0)
         load_x(1)
         multiply(1, (0,))
         transposes(2)
-        sort_words(3)
+        if SORTED_FROM <= 3:
+            sort_words(3)
         banks_out(2)
         multiply(0, (1,))
         fill("V", 1)
@@ -383,18 +394,17 @@ def tile_qdense_v_kernel(tc, x, W_rr, W_ri, W_rj, W_rk, b_rr, b_ri, b_rj, b_rk, 
             nv, ns, nd = FILL[t - 2]
             transposes(t + 1)
             fill("V")
-            drain()
             banks_out(t + 1)
             if t == 2:
                 out0(1, 0, "S")
             out0(t - 1, 1, "S")
-            if t + 2 < 8:
+            if SORTED_FROM <= t + 2 < 8:
                 sort_words(t + 2)
             gt_quantize(t + 1, 0, 4)
+            gt_quantize(t + 1, 4, 4)
             drain()
             fill("V", nv - 1)
-            gt_quantize(t + 1, 4, 4)
-            drain(nd - 2)
+            drain(nd - 1)
             multiply(t, (0, 1), (0,))
             fill("S", ns)
             out0(t, 0, "S")
@@ -419,5 +429,5 @@ def tile_qdense_v_kernel(tc, x, W_rr, W_ri, W_rj, W_rk, b_rr, b_ri, b_rj, b_rk, 
         grad_w_out(2, "S")
         grad_w_out(1, "V")
         grad_w_out(3, "S")
-        for n in range(4):
-            grad_w_store(n, ("ob00", "ob01", "ob10", "ob11")[n], "VS"[n % 2])
+        for f in range(8):
+            grad_w_store(f, "VS"[f % 2])

from contextlib import ExitStack

import concourse.mybir as mybir
from concourse.masks import make_identity

FLOPS = 2 * 20 * 1024 * 1024 * 256
BYTES = 2 * (1024 * 1024 + 4 * 1024 * 256 + 1024 * 4096) + 4 * (1024 * 1024 + 1024 * 256)

F32 = mybir.dt.float32
BF16 = mybir.dt.bfloat16
U32 = mybir.dt.uint32
U8 = mybir.dt.uint8
E4 = mybir.dt.float8_e4m3fn_x4
E5 = mybir.dt.float8_e5m2_x4
COPY = mybir.ActivationFunctionType.Copy
MULT = mybir.AluOpType.mult

P = 128
PACK = 4
KP = P * PACK
CH = 1024
IQ = 256

POS_BLOCK = {"ri": 0, "rr": 1, "rk": 3, "rj": 4}
NEG_BLOCK = {"ri": 2, "rk": 5, "rj": 6}
W_ORDER = ("ri", "rr", "rk", "rj")
WIN_RI = (1, 0, 4, 3)
WIN_KJ = (5, 6, 0, 1)
X_FOR_G = (1, 0, 3, 2)
X_SIGN = (1, -1, -1, 1)

SORTED_FROM = 3
FAST = True
FILL = ((2, 1, 3), (1, 1, 3), (2, 1, 3), (1, 1, 3), (2, 1, 3))
TAIL = (1, 1, 1, 1)
CHUNKS = ((0, 1, 2, 3), (2, 3, 0, 1))
O1_BANKS = ("ob00", "ob01", "ob10", "ob11", "xb0", "xb2", "ob00", "ob01")


def tile_qdense_v_kernel(tc, x, W_rr, W_ri, W_rj, W_rk, b_rr, b_ri, b_rj, b_rk, grad_out, out_0, out_1):
    nc = tc.nc
    weights = {"rr": W_rr, "ri": W_ri, "rj": W_rj, "rk": W_rk}

    with ExitStack() as ctx:
        keep = ctx.enter_context(tc.tile_pool(name="keep", bufs=1))
        work = ctx.enter_context(tc.tile_pool(name="work", bufs=1))
        psum = ctx.enter_context(tc.psum_pool(name="psum", bufs=1))
        ctx.enter_context(tc.manual_schedule())

        def sb(pool, shape, dtype, tag, bufs=1):
            return pool.tile(shape, dtype, name=tag, tag=tag, bufs=bufs, align_bytes=256)

        warm = sb(keep, [P, 2], F32, "warm")
        nc.gpsimd.memset(warm[:], 0.0)
        nc.scalar.activation(out=warm[:, 1:2], in_=warm[:, 0:1], func=COPY, scale=-1.0)
        ident = sb(keep, [P, P], F32, "ident")
        make_identity(nc, ident[:])

        g_raw = [sb(keep, [P, PACK, 4 * CH], BF16, "g_raw%d" % g) for g in range(2)]
        w_raw = [sb(work, [P, 4, PACK, IQ], BF16, "raw8", bufs=2) for q in range(2)]
        x_raw = []

        def load_w(q, first, last):
            for m in range(first, last):
                name = W_ORDER[m]
                rows = weights[name][q * KP : (q + 1) * KP, :]
                nc.sync.dma_start(out=w_raw[q][:, m, :, :], in_=rows.rearrange("(p j) w -> p j w", j=PACK))

        def load_g(t, pieces, first, last):
            g, j = divmod(t, PACK)
            rows = grad_out[g * KP : (g + 1) * KP, :].rearrange("(p j) w -> p j w", j=PACK)
            n = 4 * CH // pieces
            for c in range(first, last):
                cols = slice(c * n, (c + 1) * n)
                nc.sync.dma_start(out=g_raw[g][:, j, cols], in_=rows[:, j, cols])

        load_w(0, 0, 3)
        load_g(0, 4, 0, 1)
        load_w(0, 3, 4)
        load_g(0, 4, 1, 4)
        load_g(1, 4, 0, 4)
        load_w(1, 0, 4)
        for t in range(2, 8):
            load_g(t, 1, 0, 1)

        def load_x(g):
            tile = sb(work, [P, PACK, 4 * IQ], BF16, "raw8", bufs=2)
            rows = x[g * KP : (g + 1) * KP, :].rearrange("(p j) w -> p j w", j=PACK)
            nc.sync.dma_start(out=tile[:], in_=rows)
            x_raw.append(tile)

        def interleave(engine, dst, src, sign=1):
            if FAST:
                o = dst.rearrange("p (c i) t -> p c t i", i=4)
                i = src.rearrange("p t (c i) -> p c t i", i=4)
            else:
                o = dst
                i = src.rearrange("p t c -> p c t")
            if engine == "V":
                if sign > 0:
                    nc.vector.tensor_copy(out=o, in_=i)
                else:
                    nc.vector.tensor_scalar(out=o, in0=i, scalar1=-1.0, scalar2=None, op0=MULT)
            elif sign > 0:
                nc.scalar.copy(out=o, in_=i)
            else:
                nc.scalar.activation(out=o, in_=i, func=COPY, scale=-1.0)

        def quantize(codes, scales, src, fmt):
            nc.vector.quantize_mx(out=codes.bitcast(fmt), scales=scales, in_=src)

        w_il = [sb(work, [P, 7, IQ, PACK], BF16, "big16", bufs=2) for q in range(2)]
        w_codes = [sb(keep, [P, 8 * IQ], U32, "w_codes%d" % q) for q in range(2)]
        w_scales = [sb(keep, [P, 8 * IQ], U8, "w_scales%d" % q) for q in range(2)]

        def w_interleave(q, name, sign, engine):
            block = (POS_BLOCK if sign > 0 else NEG_BLOCK)[name]
            interleave(engine, w_il[q][:, block, :, :], w_raw[q][:, W_ORDER.index(name), :, :], sign)

        def w_quantize(q, first, count, src):
            cols = slice(first * IQ, (first + count) * IQ)
            quantize(
                w_codes[q][:, cols],
                w_scales[q][:, cols],
                w_il[q][:, src : src + count, :, :].rearrange("p b w j -> p (b w j)"),
                E4,
            )

        def w_negate(q, name):
            nc.vector.tensor_scalar(
                out=w_il[q][:, NEG_BLOCK[name], :, :],
                in0=w_il[q][:, POS_BLOCK[name], :, :],
                scalar1=-1.0,
                scalar2=None,
                op0=MULT,
            )

        gt = {}
        gt_codes = {}
        gt_scales = {}
        xbanks = {}
        sorted_words = {}

        def sort_words(t):
            g, j = divmod(t, PACK)
            sorted_words[t] = sb(work, [P, 4 * CH // 2], F32, "sorted", bufs=2)
            nc.vector.tensor_copy(
                out=sorted_words[t][:].rearrange("p (s u n) -> p s u n", u=2, n=P),
                in_=g_raw[g][:, j, :].bitcast(F32).rearrange("p (s n u) -> p s u n", u=2, n=P),
            )

        def transposes(t, chunks=range(4)):
            g, j = divmod(t, PACK)
            words = sorted_words[t][:] if t in sorted_words else g_raw[g][:, j, :].bitcast(F32)
            for c in chunks:
                bank = psum.tile([P, 2, 2, P], F32, name="xb%d" % c, tag="xb%d" % c, bufs=1)
                xbanks[t, c] = bank
                for q in range(2):
                    for u in range(2):
                        base = 2 * P * (2 * c + q)
                        if t in sorted_words:
                            src = words[:, base + u * P : base + (u + 1) * P]
                        else:
                            src = words[:, base + u : base + 2 * P : 2]
                        nc.tensor.transpose(bank[:, q, u, :], src, ident[:])

        def bank_out(t, c, engine):
            if t not in gt:
                gt[t] = sb(work, [P, 8, P, PACK], BF16, "gt", bufs=2)
            dst = gt[t][:, 2 * c : 2 * c + 2, :, :].rearrange("p s n i -> p s (n i)").bitcast(F32)
            dst = dst.rearrange("p s (n u) -> p s n u", u=2)
            src = xbanks[t, c][:].rearrange("p s u n -> p s n u")
            if engine == "V":
                nc.vector.tensor_copy(out=dst, in_=src)
            else:
                nc.scalar.copy(out=dst, in_=src)

        def gt_quantize(t, first, count):
            if t not in gt_codes:
                gt_codes[t] = sb(work, [P, 8 * P], U32, "gt_codes", bufs=3)
                gt_scales[t] = sb(work, [P, 8 * P], U8, "gt_scales", bufs=3)
            cols = slice(first * P, (first + count) * P)
            quantize(
                gt_codes[t][:, cols],
                gt_scales[t][:, cols],
                gt[t][:, first : first + count, :, :].rearrange("p s n i -> p (s n i)"),
                E5,
            )

        obanks = {}

        def multiply(t, halves, windows=(0, 1)):
            for b in windows:
                if (t, b) not in obanks:
                    tag = "ob%d%d" % (t % 2, b)
                    obanks[t, b] = psum.tile([P, 512], F32, name=tag, tag=tag, bufs=1)
                for n, c in enumerate(CHUNKS[b]):
                    for q in halves:
                        s = slice((2 * c + q) * P, (2 * c + q + 1) * P)
                        first = (WIN_RI, WIN_KJ)[b][c] * IQ
                        w = slice(first, first + 512)
                        nc.tensor.matmul_mx(
                            out=obanks[t, b][:],
                            lhsT=gt_codes[t][:, s].bitcast(E5),
                            lhsT_scale=gt_scales[t][:, s],
                            rhs=w_codes[q][:, w].bitcast(E4),
                            rhs_scale=w_scales[q][:, w],
                            start=(n == 0 and q == 0),
                            stop=(n == 3 and q == 1),
                        )

        o_sb = {}

        def copy(engine, out, in_):
            if engine == "V":
                nc.vector.tensor_copy(out=out, in_=in_)
            else:
                nc.scalar.copy(out=out, in_=in_)

        def out0(t, b, engine):
            g, j = divmod(t, PACK)
            if t not in o_sb:
                o_sb[t] = sb(work, [P, 4 * IQ], F32, "o_sb", bufs=3)
            if b == 0:
                copy(engine, o_sb[t][:, 0:512], obanks[t, 0][:])
            else:
                copy(engine, o_sb[t][:, 768:1024], obanks[t, 1][:, 0:256])
                copy(engine, o_sb[t][:, 512:768], obanks[t, 1][:, 256:512])
            rows = out_0[g * KP : (g + 1) * KP, :].rearrange("(p j) w -> p j w", j=PACK)
            cols = slice(b * 512, (b + 1) * 512)
            nc.sync.dma_start(out=rows[:, j, cols], in_=o_sb[t][:, cols])

        tok_codes = []
        tok_scales = []
        x_codes = []
        x_scales = []
        il = {}

        def tok_interleave(u, engine):
            g, part = divmod(u, 8)
            il[u] = sb(work, [P, 512, PACK], BF16, "il", bufs=4)
            interleave(engine, il[u][:], g_raw[g][:, :, part * 512 : (part + 1) * 512])

        def tok_quantize(u):
            g, part = divmod(u, 8)
            if part == 0:
                if g == 0:
                    tok_codes.append(sb(keep, [P, 4 * CH], U32, "tok_codes0"))
                else:
                    tok_codes.append(sb(work, [P, 4 * CH], U32, "big16", bufs=2))
                tok_scales.append(sb(keep, [P, 4 * CH], U8, "tok_scales%d" % g))
            cols = slice(part * 512, (part + 1) * 512)
            quantize(tok_codes[g][:, cols], tok_scales[g][:, cols], il[u][:].rearrange("p n i -> p (n i)"), E5)

        x_il = {}

        def x_interleave(g, c, engine):
            pair = c // 2
            if c % 2 == 0:
                x_il[g, pair] = sb(work, [P, 512, PACK], BF16, "il", bufs=4)
            half = slice((c % 2) * IQ, (c % 2 + 1) * IQ)
            interleave(engine, x_il[g, pair][:, half, :], x_raw[g][:, :, c * IQ : (c + 1) * IQ], X_SIGN[c])

        def x_quantize(g, pair):
            if g == 0 and pair == 0:
                x_codes.append(sb(work, [P, 2, 4 * IQ], U32, "big16", bufs=2))
                x_scales.append(sb(keep, [P, 2, 4 * IQ], U8, "x_scales"))
            cols = slice(pair * 512, (pair + 1) * 512)
            quantize(
                x_codes[0][:, g, cols], x_scales[0][:, g, cols], x_il[g, pair][:].rearrange("p n i -> p (n i)"), E4
            )

        nbanks = {}

        def grad_w(h):
            for i in range(2):
                k = 2 * i + h
                nbanks[k] = psum.tile([P, 512], F32, name="xb%d" % k, tag="xb%d" % k, bufs=1)
                for g in range(2):
                    for c in range(4):
                        xs = slice(X_FOR_G[c] * IQ + i * P, X_FOR_G[c] * IQ + (i + 1) * P)
                        gs = slice(c * CH + h * 512, c * CH + (h + 1) * 512)
                        nc.tensor.matmul_mx(
                            out=nbanks[k][:],
                            lhsT=x_codes[0][:, g, xs].bitcast(E4),
                            lhsT_scale=x_scales[0][:, g, xs],
                            rhs=tok_codes[g][:, gs].bitcast(E5),
                            rhs_scale=tok_scales[g][:, gs],
                            start=(g == 0 and c == 0),
                            stop=(g == 1 and c == 3),
                        )

        o1t = {}
        o1 = []

        def grad_w_out(k, engine):
            o1t[k] = sb(work, [P, 512], F32, "il", bufs=4)
            copy(engine, o1t[k][:], nbanks[k][:])

        def grad_w_store(f, engine):
            tag = O1_BANKS[f]
            bank = psum.tile([P, 2, P], F32, name=tag, tag=tag, bufs=1)
            h, part = divmod(f, 4)
            for i in range(2):
                nc.tensor.transpose(bank[:, i, :], o1t[2 * i + h][:, part * P : (part + 1) * P], ident[:])
            if f == 0:
                o1.append(sb(work, [P, 8, 2 * P], F32, "gt", bufs=2))
            res = o1[0][:, f, :]
            copy(engine, res, bank[:].rearrange("p i n -> p (i n)"))
            nc.sync.dma_start(out=out_1[f * P : (f + 1) * P, :], in_=res)

        items = [("t", u) for u in (0, 2, 4, 6, 1, 3, 5, 7)] + [("x", c) for c in range(4)]
        items += [("t", u) for u in (8, 10, 12, 14)] + [("x", c) for c in range(4, 8)]
        items += [("t", u) for u in (9, 11, 13, 15)]
        pending = []

        def fill(engine, count=1):
            share = 2 * count
            while items and share > 0:
                kind, n = items.pop(0)
                share -= 2 if kind == "t" else 1
                if kind == "t":
                    tok_interleave(n, engine)
                    pending.append((kind, n))
                else:
                    x_interleave(n // 4, n % 4, engine)
                    if n % 2 == 1:
                        pending.append((kind, n // 2))

        def drain(count=1):
            for k in range(count):
                if not pending:
                    return
                kind, n = pending.pop(0)
                if kind == "t":
                    tok_quantize(n)
                else:
                    x_quantize(n // 2, n % 2)

        def banks_out(t, engine="S"):
            for c in range(4):
                bank_out(t, c, engine)

        w_interleave(0, "ri", 1, "V")
        w_interleave(0, "ri", -1, "S")
        w_interleave(0, "rr", 1, "V")
        w_interleave(0, "rk", 1, "V")
        w_quantize(0, 0, 2, 0)
        w_interleave(0, "rk", -1, "S")
        w_interleave(0, "rj", 1, "V")
        w_quantize(0, 2, 1, 2)
        w_negate(0, "rj")
        transposes(0)
        banks_out(0)
        gt_quantize(0, 0, 4)
        w_quantize(0, 3, 2, 3)
        gt_quantize(0, 4, 4)
        w_quantize(0, 7, 1, 3)
        w_quantize(0, 5, 2, 5)
        transposes(1)
        banks_out(1)
        multiply(0, (0,))
        gt_quantize(1, 0, 4)
        w_interleave(1, "ri", 1, "V")
        gt_quantize(1, 4, 4)
        w_interleave(1, "rj", 1, "S")
        w_interleave(1, "rr", 1, "V")
        w_interleave(1, "ri", -1, "S")
        w_interleave(1, "rk", 1, "V")
        w_interleave(1, "rk", -1, "S")
        w_quantize(1, 0, 2, 0)
        w_quantize(1, 3, 2, 3)
        w_negate(1, "rj")
        w_quantize(1, 7, 1, 3)
        w_quantize(1, 2, 1, 2)
        w_quantize(1, 5, 2, 5)
        load_x(0)
        load_x(1)
        multiply(1, (0,))
        transposes(2)
        if SORTED_FROM <= 3:
            sort_words(3)
        banks_out(2)
        multiply(0, (1,))
        fill("V", 1)
        gt_quantize(2, 0, 4)
        gt_quantize(2, 4, 4)
        fill("S", 1)
        multiply(1, (1,))
        out0(0, 0, "S")
        out0(0, 1, "S")

        for t in range(2, 7):
            nv, ns, nd = FILL[t - 2]
            transposes(t + 1)
            fill("V")
            banks_out(t + 1)
            if t == 2:
                out0(1, 0, "S")
            out0(t - 1, 1, "S")
            if SORTED_FROM <= t + 2 < 8:
                sort_words(t + 2)
            gt_quantize(t + 1, 0, 4)
            gt_quantize(t + 1, 4, 4)
            drain()
            fill("V", nv - 1)
            drain(nd - 1)
            multiply(t, (0, 1), (0,))
            fill("S", ns)
            out0(t, 0, "S")
            multiply(t, (0, 1), (1,))
        multiply(7, (0, 1), (0,))
        fill("V", TAIL[0])
        drain(1)
        fill("S", TAIL[1])
        out0(6, 1, "S")
        drain(2)
        fill("V", TAIL[2])
        drain(2)
        out0(7, 0, "S")
        multiply(7, (0, 1), (1,))
        fill("S", TAIL[3])
        fill("V", 9)
        drain(9)
        out0(7, 1, "S")
        grad_w(0)
        grad_w(1)
        grad_w_out(0, "V")
        grad_w_out(2, "S")
        grad_w_out(1, "V")
        grad_w_out(3, "S")
        for f in range(8):
            grad_w_store(f, "VS"[f % 2])
